import numpy as np
import ml_dtypes


def mxq(x, axis, fmt="e4m3"):
    dtype, down = {"e4m3": (ml_dtypes.float8_e4m3fn, 7), "e5m2": (ml_dtypes.float8_e5m2, 14)}[fmt]
    v = np.moveaxis(np.asarray(x, np.float32).astype(ml_dtypes.bfloat16).astype(np.float64), axis, -1)
    blocks = v.reshape(v.shape[:-1] + (-1, 32))
    amax = np.abs(blocks).max(-1, keepdims=True)
    byte = np.maximum(np.where(amax > 0, np.frexp(amax)[1] - 1 + 127, 0) - down, 1)
    scale = np.exp2(byte - 127.0)
    codes = (blocks / scale).astype(np.float32).astype(dtype).astype(np.float64)
    return np.moveaxis((codes * scale).reshape(v.shape), -1, axis)


WIDE = False


def mx_kscale(k):
    if not WIDE:
        return np.ones(k)
    levels = np.array([20, -20, 10, -10, 0])
    a = np.random.permutation(np.resize(levels, k // 512 * 4)).reshape(k // 512, 4)
    idx = np.arange(k)
    return np.exp2(a[idx // 512, idx % 128 // 32])


BF16 = ml_dtypes.bfloat16


def bf(x):
    return np.asarray(x, np.float32).astype(BF16)


def f64(x):
    return np.asarray(x).astype(np.float64)


B, C, O, H, W = 512, 128, 512, 3, 3
KH, KW, PAD = 3, 3, 1


def setup_inputs():
    s = mx_kscale(B)[:, None, None, None]
    x = np.random.standard_normal((B, C, H, W)) * s
    weight = np.random.standard_normal((1, O, C, H, W, KH * KW)) / np.sqrt(KH * KW * C)
    g = np.random.standard_normal((B, O, H, W)) * np.exp2(np.random.randint(-12, 1, (B, 1, H, W))) / s
    return {"x": bf(x), "weight": bf(weight), "grad_out": bf(g)}


def reference(x, weight, grad_out):
    xq = mxq(f64(x), 0, "e4m3")
    gq = mxq(f64(grad_out), 0, "e5m2")
    out = np.zeros((1, O, C, H, W, KH * KW))
    for i in range(KH):
        for j in range(KW):
            h0, h1 = max(0, PAD - i), min(H, H + PAD - i)
            w0, w1 = max(0, PAD - j), min(W, W + PAD - j)
            gs = gq[:, :, h0:h1, w0:w1]
            xs = xq[:, :, h0 + i - PAD:h1 + i - PAD, w0 + j - PAD:w1 + j - PAD]
            p = gs.transpose(2, 3, 1, 0) @ xs.transpose(2, 3, 0, 1)
            out[0, :, :, h0:h1, w0:w1, i * KW + j] = p.transpose(2, 3, 0, 1)
    return out

@@ -1,0 +1,177 @@
+from contextlib import ExitStack
+
+import concourse.mybir as mybir
+
+F32 = mybir.dt.float32
+BF16 = mybir.dt.bfloat16
+U32 = mybir.dt.uint32
+U8 = mybir.dt.uint8
+E4X4 = mybir.dt.float8_e4m3fn_x4
+E5X4 = mybir.dt.float8_e5m2_x4
+
+P = 128
+PACK = 4
+B, C, O = 512, 128, 512
+GRID = 9
+XCOLS = C * GRID
+GCOLS = P * GRID
+OBLOCKS = O // P
+N_PASS = 512
+RUN = GRID * GRID
+
+FLOPS = 2 * 49 * B * C * O
+BYTES = 2 * B * XCOLS + 2 * B * O * GRID + 4 * O * C * RUN
+
+RANGES = ((0, 48, 0, "s"), (48, 96, 384, "s"), (96, 128, 640, "v"))
+X_CHUNKS = ((0, 172), (172, 344), (344, 384))
+X_PIECES = ((0, 512), (512, 1024), (1024, 1152))
+N_S = 4
+N_V = 2
+
+
+def tile_locallyconnected2d_kernel(tc, x, weight, grad_out, out):
+    nc = tc.nc
+    x_v = x.rearrange("(p j) c h w -> p j (c h w)", j=PACK)
+    g_v = grad_out.rearrange("(p j) o h w -> p j (o h w)", j=PACK)
+    out_v = out.rearrange("a (b o) c h w t -> (a b) o c (h w t)", o=P)
+
+    with ExitStack() as ctx:
+        keep = ctx.enter_context(tc.tile_pool(name="keep", bufs=1))
+        gpool = ctx.enter_context(tc.tile_pool(name="gpool", bufs=2))
+        ps_s = ctx.enter_context(tc.psum_pool(name="ps_s", bufs=5))
+        ps_v = ctx.enter_context(tc.psum_pool(name="ps_v", bufs=3))
+
+        xraw = keep.tile([P, PACK, XCOLS], BF16, name="xraw")
+        nc.sync.dma_start(out=xraw[:], in_=x_v)
+        graw = []
+        for ob in range(OBLOCKS):
+            t = keep.tile([P, PACK, GCOLS], BF16, name="graw%d" % ob)
+            nc.sync.dma_start(out=t[:], in_=g_v[:, :, ob * GCOLS:(ob + 1) * GCOLS])
+            graw.append(t)
+
+        xg = []
+        for w in range(3):
+            t = keep.tile([P, XCOLS, PACK], BF16, name="xg%d" % w, align_bytes=64)
+            xg.append(t)
+        xc = keep.tile([P, 3, XCOLS], U32, name="xc", align_bytes=64)
+        xs = keep.tile([P, 3, XCOLS], U8, name="xs", align_bytes=64)
+        gc = keep.tile([P, OBLOCKS, GCOLS], U32, name="gc", align_bytes=64)
+        gs = keep.tile([P, OBLOCKS, GCOLS], U8, name="gs", align_bytes=64)
+        zero = keep.tile([P, 21], F32, name="zero")
+
+        n_s = RANGES[0][1] - RANGES[0][0]
+        n_v = RANGES[2][1] - RANGES[2][0]
+        st_s = []
+        for i in range(N_S):
+            t = keep.tile([P, n_s, RUN], F32, name="st_s%d" % i)
+            st_s.append(t)
+        st_v = []
+        for i in range(N_V):
+            t = keep.tile([P, n_v, RUN], F32, name="st_v%d" % i)
+            st_v.append(t)
+
+        nc.vector.memset(zero[:], 0.0)
+        nc.vector.memset(xg[0][:], 0.0)
+        nc.vector.memset(xg[2][:], 0.0)
+        for t in st_v:
+            nc.vector.memset(t[:, :, 0:21], 0.0)
+            nc.vector.memset(t[:, :, 60:81], 0.0)
+
+        def zero_s(t):
+            src = zero[:].unsqueeze(1).to_broadcast([P, n_s, 21])
+            nc.scalar.copy(out=t[:, :, 0:21], in_=src)
+            nc.scalar.copy(out=t[:, :, 60:81], in_=src)
+
+        zero_s(st_s[0])
+        zero_s(st_s[1])
+
+        def x_regroup(k):
+            r0, r1 = X_CHUNKS[k]
+            nc.vector.tensor_copy(
+                out=xg[1][:, 3 * r0:3 * r1, :].rearrange("p (c i) t -> p c t i", i=4),
+                in_=xraw[:, :, 3 * r0:3 * r1].rearrange("p t (c i) -> p c t i", i=4),
+            )
+            raw4 = xraw[:].rearrange("p t (r w) -> p t r w", w=3)
+            for w, dst0, src0 in ((0, 1, 0), (2, 0, 1)):
+                g4 = xg[w][:].rearrange("p (r w) t -> p r w t", w=3)
+                nc.scalar.copy(
+                    out=g4[:, r0:r1, dst0:dst0 + 2, :].rearrange("p r w t -> p r t w"),
+                    in_=raw4[:, :, r0:r1, src0:src0 + 2].rearrange("p t r w -> p r t w"),
+                )
+
+        def x_quantise(k):
+            a, b = X_PIECES[k]
+            for w in (1, 0, 2):
+                nc.vector.quantize_mx(
+                    out=xc[:, w, a:b].bitcast(E4X4),
+                    scales=xs[:, w, a:b],
+                    in_=xg[w][:, a:b, :].rearrange("p n j -> p (n j)"),
+                )
+
+        def g_prepare(ob):
+            gg = gpool.tile([P, GRID, P, PACK], BF16, name="gg", align_bytes=64)
+            raw4 = graw[ob][:].rearrange("p j (o s) -> p o j s", s=GRID)
+            for s0 in (0, 3, 6):
+                nc.vector.tensor_copy(
+                    out=gg[:, s0:s0 + 3, :, :].rearrange("p s o j -> p o j s"),
+                    in_=raw4[:, :, :, s0:s0 + 3],
+                )
+            for a, b in ((0, 8), (8, 9)):
+                nc.vector.quantize_mx(
+                    out=gc[:, ob, a * P:b * P].bitcast(E5X4),
+                    scales=gs[:, ob, a * P:b * P],
+                    in_=gg[:, a:b, :, :].rearrange("p s o j -> p (s o j)"),
+                )
+
+        x_regroup(0)
+        x_quantise(0)
+        g_prepare(0)
+        x_regroup(1)
+        x_regroup(2)
+        x_quantise(1)
+        x_quantise(2)
+        zero_s(st_s[2])
+        zero_s(st_s[3])
+
+        def product(ob, rng, place, stage):
+            c0, c1, col0, eng = rng
+            h, w = divmod(place, 3)
+            pool = ps_s if eng == "s" else ps_v
+            acc = pool.tile([P, N_PASS], F32, name="acc_" + eng)
+            nc.tensor.matmul_mx(
+                out=acc[:],
+                lhsT=gc[:, ob, place * P:(place + 1) * P].bitcast(E5X4),
+                lhsT_scale=gs[:, ob, place * P:(place + 1) * P],
+                rhs=xc[:, w, col0:col0 + N_PASS].bitcast(E4X4),
+                rhs_scale=xs[:, w, col0:col0 + N_PASS],
+                start=True,
+                stop=True,
+            )
+            s_lo, s_hi, t_lo = ((0, 6, 3), (0, 9, 0), (3, 9, 0))[h]
+            src = acc[:, GRID * c0 - col0:GRID * c1 - col0].rearrange("p (c s) -> p c s", s=GRID)
+            dst = stage[:, :, place * GRID + t_lo:place * GRID + t_lo + s_hi - s_lo]
+            if eng == "s":
+                nc.scalar.copy(out=dst, in_=src[:, :, s_lo:s_hi])
+            else:
+                nc.vector.tensor_copy(out=dst, in_=src[:, :, s_lo:s_hi])
+
+        def store(ob, rng, stage):
+            nc.sync.dma_start(out=out_v[ob, :, rng[0]:rng[1], :], in_=stage[:])
+
+        for ob in range(OBLOCKS):
+            if ob + 1 < OBLOCKS:
+                g_prepare(ob + 1)
+            sa = st_s[(2 * ob) % N_S]
+            sb = st_s[(2 * ob + 1) % N_S]
+            sv = st_v[ob % N_V]
+            for i in range(GRID):
+                for k in (2 * i, 2 * i + 1):
+                    if k < GRID:
+                        product(ob, RANGES[0], k, sa)
+                    else:
+                        product(ob, RANGES[1], k - GRID, sb)
+                    if k == GRID - 1:
+                        store(ob, RANGES[0], sa)
+                product(ob, RANGES[2], i, sv)
+            store(ob, RANGES[1], sb)
+            store(ob, RANGES[2], sv)

@@ -8,25 +8,32 @@ U32 = mybir.dt.uint32
 U8 = mybir.dt.uint8
 E4X4 = mybir.dt.float8_e4m3fn_x4
 E5X4 = mybir.dt.float8_e5m2_x4
+MULT = mybir.AluOpType.mult
+ADD = mybir.AluOpType.add
 
 P = 128
 PACK = 4
 B, C, O = 512, 128, 512
 GRID = 9
+RUN = GRID * GRID
 XCOLS = C * GRID
 GCOLS = P * GRID
 OBLOCKS = O // P
 N_PASS = 512
-RUN = GRID * GRID
+CR = 32
+NR = C // CR
+XR = CR * GRID
+USED = CR * 12
 
 FLOPS = 2 * 49 * B * C * O
 BYTES = 2 * B * XCOLS + 2 * B * O * GRID + 4 * O * C * RUN
 
-RANGES = ((0, 48, 0, "s"), (48, 96, 384, "s"), (96, 128, 640, "v"))
-X_CHUNKS = ((0, 172), (172, 344), (344, 384))
-X_PIECES = ((0, 512), (512, 1024), (1024, 1152))
-N_S = 4
-N_V = 2
+S_TILES = ((0, 0), (0, 1), (0, 2), (0, 3), (1, 1), (1, 3), (2, 1), (2, 3), (3, 1), (3, 3))
+V_TILES = ((1, 0), (1, 2), (2, 0), (2, 2), (3, 0), (3, 2))
+V_START = 31
+N_S = 5
+N_V = 3
+GPSIMD_BLOCKS = (2, 3)
 
 
 def tile_locallyconnected2d_kernel(tc, x, weight, grad_out, out):
@@ -37,104 +44,110 @@ def tile_locallyconnected2d_kernel(tc, x, weight, grad_out, out):
 
     with ExitStack() as ctx:
         keep = ctx.enter_context(tc.tile_pool(name="keep", bufs=1))
-        gpool = ctx.enter_context(tc.tile_pool(name="gpool", bufs=2))
         ps_s = ctx.enter_context(tc.psum_pool(name="ps_s", bufs=5))
         ps_v = ctx.enter_context(tc.psum_pool(name="ps_v", bufs=3))
+        ctx.enter_context(tc.manual_schedule())
 
         xraw = keep.tile([P, PACK, XCOLS], BF16, name="xraw")
-        nc.sync.dma_start(out=xraw[:], in_=x_v)
-        graw = []
-        for ob in range(OBLOCKS):
-            t = keep.tile([P, PACK, GCOLS], BF16, name="graw%d" % ob)
-            nc.sync.dma_start(out=t[:], in_=g_v[:, :, ob * GCOLS:(ob + 1) * GCOLS])
-            graw.append(t)
-
-        xg = []
-        for w in range(3):
-            t = keep.tile([P, XCOLS, PACK], BF16, name="xg%d" % w, align_bytes=64)
-            xg.append(t)
-        xc = keep.tile([P, 3, XCOLS], U32, name="xc", align_bytes=64)
-        xs = keep.tile([P, 3, XCOLS], U8, name="xs", align_bytes=64)
+        xg = keep.tile([P, NR, N_PASS, PACK], BF16, name="xg", align_bytes=64)
+        xc = keep.tile([P, NR * N_PASS], U32, name="xc", align_bytes=64)
+        xs = keep.tile([P, NR * N_PASS], U8, name="xs", align_bytes=64)
         gc = keep.tile([P, OBLOCKS, GCOLS], U32, name="gc", align_bytes=64)
         gs = keep.tile([P, OBLOCKS, GCOLS], U8, name="gs", align_bytes=64)
         zero = keep.tile([P, 21], F32, name="zero")
+        graw = []
+        gg = []
+        for ob in range(OBLOCKS):
+            t = keep.tile([P, PACK, GCOLS], BF16, name="graw%d" % ob)
+            graw.append(t)
+            t = keep.tile([P, GRID, P, PACK], BF16, name="gg%d" % ob, align_bytes=64)
+            gg.append(t)
+        st = {"s": [], "v": []}
+        for eng, n in (("s", N_S), ("v", N_V)):
+            for i in range(n):
+                t = keep.tile([P, CR, RUN], F32, name="st_%s%d" % (eng, i))
+                st[eng].append(t)
 
-        n_s = RANGES[0][1] - RANGES[0][0]
-        n_v = RANGES[2][1] - RANGES[2][0]
-        st_s = []
-        for i in range(N_S):
-            t = keep.tile([P, n_s, RUN], F32, name="st_s%d" % i)
-            st_s.append(t)
-        st_v = []
-        for i in range(N_V):
-            t = keep.tile([P, n_v, RUN], F32, name="st_v%d" % i)
-            st_v.append(t)
+        nc.sync.dma_start(out=xraw[:, :, 0:XR], in_=x_v[:, :, 0:XR])
+        nc.sync.dma_start(out=graw[0][:], in_=g_v[:, :, 0:GCOLS])
+        nc.sync.dma_start(out=xraw[:, :, XR:XCOLS], in_=x_v[:, :, XR:XCOLS])
+        for ob in range(1, OBLOCKS):
+            nc.sync.dma_start(out=graw[ob][:], in_=g_v[:, :, ob * GCOLS:(ob + 1) * GCOLS])
 
+        for r in range(NR):
+            nc.gpsimd.memset(xg[:, r, :, :].rearrange("p n j -> p (n j)").bitcast(F32), 0.0)
         nc.vector.memset(zero[:], 0.0)
-        nc.vector.memset(xg[0][:], 0.0)
-        nc.vector.memset(xg[2][:], 0.0)
-        for t in st_v:
+        for t in st["v"]:
             nc.vector.memset(t[:, :, 0:21], 0.0)
             nc.vector.memset(t[:, :, 60:81], 0.0)
+        zsrc = zero[:].unsqueeze(1).to_broadcast([P, CR, 21])
+        for t in st["s"]:
+            nc.scalar.copy(out=t[:, :, 0:21], in_=zsrc)
+            nc.scalar.copy(out=t[:, :, 60:81], in_=zsrc)
 
-        def zero_s(t):
-            src = zero[:].unsqueeze(1).to_broadcast([P, n_s, 21])
-            nc.scalar.copy(out=t[:, :, 0:21], in_=src)
-            nc.scalar.copy(out=t[:, :, 60:81], in_=src)
+        def x_regroup(r):
+            dst = xg[:, r, 0:USED, :].rearrange("p (q k) j -> p q k j", k=4)[:, :, 1:4, :]
+            src = xraw[:, :, r * XR:(r + 1) * XR].rearrange("p j (q w) -> p q j w", w=3)
+            nc.vector.tensor_copy(out=dst.rearrange("p q k j -> p q j k"), in_=src)
 
-        zero_s(st_s[0])
-        zero_s(st_s[1])
-
-        def x_regroup(k):
-            r0, r1 = X_CHUNKS[k]
-            nc.vector.tensor_copy(
-                out=xg[1][:, 3 * r0:3 * r1, :].rearrange("p (c i) t -> p c t i", i=4),
-                in_=xraw[:, :, 3 * r0:3 * r1].rearrange("p t (c i) -> p c t i", i=4),
+        def x_quantise(r):
+            nc.vector.quantize_mx(
+                out=xc[:, r * N_PASS:(r + 1) * N_PASS].bitcast(E4X4),
+                scales=xs[:, r * N_PASS:(r + 1) * N_PASS],
+                in_=xg[:, r, :, :].rearrange("p n j -> p (n j)"),
             )
-            raw4 = xraw[:].rearrange("p t (r w) -> p t r w", w=3)
-            for w, dst0, src0 in ((0, 1, 0), (2, 0, 1)):
-                g4 = xg[w][:].rearrange("p (r w) t -> p r w t", w=3)
-                nc.scalar.copy(
-                    out=g4[:, r0:r1, dst0:dst0 + 2, :].rearrange("p r w t -> p r t w"),
-                    in_=raw4[:, :, r0:r1, src0:src0 + 2].rearrange("p t r w -> p r t w"),
-                )
 
-        def x_quantise(k):
-            a, b = X_PIECES[k]
-            for w in (1, 0, 2):
-                nc.vector.quantize_mx(
-                    out=xc[:, w, a:b].bitcast(E4X4),
-                    scales=xs[:, w, a:b],
-                    in_=xg[w][:, a:b, :].rearrange("p n j -> p (n j)"),
-                )
+        def g_regroup(ob, s0, s1, o0, o1, eng):
+            dst = gg[ob][:, s0:s1, o0:o1, :].rearrange("p s o j -> p o j s")
+            src = graw[ob][:].rearrange("p j (o s) -> p o j s", s=GRID)[:, o0:o1, :, s0:s1]
+            if eng == "v":
+                nc.vector.tensor_copy(out=dst, in_=src)
+            else:
+                nc.gpsimd.tensor_scalar(out=dst, in0=src, scalar1=1.0, scalar2=0.0, op0=MULT, op1=ADD)
 
-        def g_prepare(ob):
-            gg = gpool.tile([P, GRID, P, PACK], BF16, name="gg", align_bytes=64)
-            raw4 = graw[ob][:].rearrange("p j (o s) -> p o j s", s=GRID)
-            for s0 in (0, 3, 6):
-                nc.vector.tensor_copy(
-                    out=gg[:, s0:s0 + 3, :, :].rearrange("p s o j -> p o j s"),
-                    in_=raw4[:, :, :, s0:s0 + 3],
-                )
-            for a, b in ((0, 8), (8, 9)):
-                nc.vector.quantize_mx(
-                    out=gc[:, ob, a * P:b * P].bitcast(E5X4),
-                    scales=gs[:, ob, a * P:b * P],
-                    in_=gg[:, a:b, :, :].rearrange("p s o j -> p (s o j)"),
-                )
+        def g_quantise(ob, s0, s1):
+            nc.vector.quantize_mx(
+                out=gc[:, ob, s0 * P:s1 * P].bitcast(E5X4),
+                scales=gs[:, ob, s0 * P:s1 * P],
+                in_=gg[ob][:, s0:s1, :, :].rearrange("p s o j -> p (s o j)"),
+            )
 
         x_regroup(0)
         x_quantise(0)
-        g_prepare(0)
+        g_regroup(0, 0, 4, 0, P, "v")
+        g_regroup(0, 4, 8, 0, P, "v")
+        g_quantise(0, 0, 4)
+        g_regroup(0, 8, 9, 0, P, "v")
+        g_quantise(0, 4, 8)
         x_regroup(1)
+        g_quantise(0, 8, 9)
         x_regroup(2)
         x_quantise(1)
+        x_regroup(3)
         x_quantise(2)
-        zero_s(st_s[2])
-        zero_s(st_s[3])
+        g_regroup(1, 0, 4, 0, P, "v")
+        x_quantise(3)
+        g_regroup(1, 4, 8, 0, P, "v")
+        g_regroup(1, 8, 9, 0, P, "v")
+        g_quantise(1, 0, 8)
+        g_quantise(1, 8, 9)
 
-        def product(ob, rng, place, stage):
-            c0, c1, col0, eng = rng
+        for ob in GPSIMD_BLOCKS:
+            for s0 in (0, 4):
+                for o0 in (0, 64):
+                    g_regroup(ob, s0, s0 + 4, o0, o0 + 64, "g")
+            g_regroup(ob, 8, 9, 0, P, "g")
+
+        quantised = [0, 1]
+        count = {"s": 0, "v": 0}
+
+        def product(ob, r, place, eng):
+            if ob not in quantised:
+                g_quantise(ob, 0, 8)
+                g_quantise(ob, 8, 9)
+                quantised.append(ob)
+            stage = st[eng][(count[eng] // GRID) % len(st[eng])]
+            count[eng] = count[eng] + 1
             h, w = divmod(place, 3)
             pool = ps_s if eng == "s" else ps_v
             acc = pool.tile([P, N_PASS], F32, name="acc_" + eng)
@@ -142,36 +155,28 @@ def tile_locallyconnected2d_kernel(tc, x, weight, grad_out, out):
                 out=acc[:],
                 lhsT=gc[:, ob, place * P:(place + 1) * P].bitcast(E5X4),
                 lhsT_scale=gs[:, ob, place * P:(place + 1) * P],
-                rhs=xc[:, w, col0:col0 + N_PASS].bitcast(E4X4),
-                rhs_scale=xs[:, w, col0:col0 + N_PASS],
+                rhs=xc[:, r * N_PASS:(r + 1) * N_PASS].bitcast(E4X4),
+                rhs_scale=xs[:, r * N_PASS:(r + 1) * N_PASS],
                 start=True,
                 stop=True,
             )
-            s_lo, s_hi, t_lo = ((0, 6, 3), (0, 9, 0), (3, 9, 0))[h]
-            src = acc[:, GRID * c0 - col0:GRID * c1 - col0].rearrange("p (c s) -> p c s", s=GRID)
-            dst = stage[:, :, place * GRID + t_lo:place * GRID + t_lo + s_hi - s_lo]
+            a_lo, a_hi, t_lo = ((0, 2, 3), (0, 3, 0), (1, 3, 0))[h]
+            src = acc[:, w:w + USED].rearrange("p (c a k) -> p c a k", a=3, k=4)[:, :, a_lo:a_hi, 0:3]
+            first = place * GRID + t_lo
+            dst = stage[:, :, first:first + 3 * (a_hi - a_lo)].rearrange("p c (a k) -> p c a k", k=3)
             if eng == "s":
-                nc.scalar.copy(out=dst, in_=src[:, :, s_lo:s_hi])
+                nc.scalar.copy(out=dst, in_=src)
             else:
-                nc.vector.tensor_copy(out=dst, in_=src[:, :, s_lo:s_hi])
+                nc.vector.tensor_copy(out=dst, in_=src)
+            if place == GRID - 1:
+                nc.sync.dma_start(out=out_v[ob, :, r * CR:(r + 1) * CR, :], in_=stage[:])
 
-        def store(ob, rng, stage):
-            nc.sync.dma_start(out=out_v[ob, :, rng[0]:rng[1], :], in_=stage[:])
-
-        for ob in range(OBLOCKS):
-            if ob + 1 < OBLOCKS:
-                g_prepare(ob + 1)
-            sa = st_s[(2 * ob) % N_S]
-            sb = st_s[(2 * ob + 1) % N_S]
-            sv = st_v[ob % N_V]
-            for i in range(GRID):
-                for k in (2 * i, 2 * i + 1):
-                    if k < GRID:
-                        product(ob, RANGES[0], k, sa)
-                    else:
-                        product(ob, RANGES[1], k - GRID, sb)
-                    if k == GRID - 1:
-                        store(ob, RANGES[0], sa)
-                product(ob, RANGES[2], i, sv)
-            store(ob, RANGES[1], sb)
-            store(ob, RANGES[2], sv)
+        s_units = [(ob, r, place) for ob, r in S_TILES for place in range(GRID)]
+        v_units = [(ob, r, place) for ob, r in V_TILES for place in range(GRID)]
+        for i in range(len(s_units)):
+            ob, r, place = s_units[i]
+            product(ob, r, place, "s")
+            k = i - V_START
+            if 0 <= k < len(v_units):
+                ob, r, place = v_units[k]
+                product(ob, r, place, "v")

@@ -28,12 +28,12 @@ USED = CR * 12
 FLOPS = 2 * 49 * B * C * O
 BYTES = 2 * B * XCOLS + 2 * B * O * GRID + 4 * O * C * RUN
 
-S_TILES = ((0, 0), (0, 1), (0, 2), (0, 3), (1, 1), (1, 3), (2, 1), (2, 3), (3, 1), (3, 3))
-V_TILES = ((1, 0), (1, 2), (2, 0), (2, 2), (3, 0), (3, 2))
-V_START = 31
-N_S = 5
-N_V = 3
-GPSIMD_BLOCKS = (2, 3)
+N_STAGE = 6
+S_ZEROED = 3
+TILES = tuple((ob, r) for ob in range(OBLOCKS) for r in range(NR))
+V_SHARE = {1: (5,), 2: (3, 7), 3: (1, 4, 7), 4: (1, 3, 5, 7), 5: (0, 2, 4, 6, 8)}
+V_COUNT = (1, 2, 1, 2) + (3, 4) * 4 + (4, 5) * 2
+GPSIMD_BLOCKS = ()
 
 
 def tile_locallyconnected2d_kernel(tc, x, weight, grad_out, out):
@@ -62,11 +62,10 @@ def tile_locallyconnected2d_kernel(tc, x, weight, grad_out, out):
             graw.append(t)
             t = keep.tile([P, GRID, P, PACK], BF16, name="gg%d" % ob, align_bytes=64)
             gg.append(t)
-        st = {"s": [], "v": []}
-        for eng, n in (("s", N_S), ("v", N_V)):
-            for i in range(n):
-                t = keep.tile([P, CR, RUN], F32, name="st_%s%d" % (eng, i))
-                st[eng].append(t)
+        st = []
+        for i in range(N_STAGE):
+            t = keep.tile([P, CR, RUN], F32, name="st%d" % i)
+            st.append(t)
 
         nc.sync.dma_start(out=xraw[:, :, 0:XR], in_=x_v[:, :, 0:XR])
         nc.sync.dma_start(out=graw[0][:], in_=g_v[:, :, 0:GCOLS])
@@ -77,11 +76,11 @@ def tile_locallyconnected2d_kernel(tc, x, weight, grad_out, out):
         for r in range(NR):
             nc.gpsimd.memset(xg[:, r, :, :].rearrange("p n j -> p (n j)").bitcast(F32), 0.0)
         nc.vector.memset(zero[:], 0.0)
-        for t in st["v"]:
+        for t in st[S_ZEROED:]:
             nc.vector.memset(t[:, :, 0:21], 0.0)
             nc.vector.memset(t[:, :, 60:81], 0.0)
         zsrc = zero[:].unsqueeze(1).to_broadcast([P, CR, 21])
-        for t in st["s"]:
+        for t in st[:S_ZEROED]:
             nc.scalar.copy(out=t[:, :, 0:21], in_=zsrc)
             nc.scalar.copy(out=t[:, :, 60:81], in_=zsrc)
 
@@ -102,6 +101,8 @@ def tile_locallyconnected2d_kernel(tc, x, weight, grad_out, out):
             src = graw[ob][:].rearrange("p j (o s) -> p o j s", s=GRID)[:, o0:o1, :, s0:s1]
             if eng == "v":
                 nc.vector.tensor_copy(out=dst, in_=src)
+            elif eng == "s":
+                nc.scalar.copy(out=dst, in_=src)
             else:
                 nc.gpsimd.tensor_scalar(out=dst, in0=src, scalar1=1.0, scalar2=0.0, op0=MULT, op1=ADD)
 
@@ -115,22 +116,9 @@ def tile_locallyconnected2d_kernel(tc, x, weight, grad_out, out):
         x_regroup(0)
         x_quantise(0)
         g_regroup(0, 0, 4, 0, P, "v")
-        g_regroup(0, 4, 8, 0, P, "v")
+        g_regroup(0, 4, 8, 0, P, "s")
+        g_regroup(0, 8, 9, 0, P, "s")
         g_quantise(0, 0, 4)
-        g_regroup(0, 8, 9, 0, P, "v")
-        g_quantise(0, 4, 8)
-        x_regroup(1)
-        g_quantise(0, 8, 9)
-        x_regroup(2)
-        x_quantise(1)
-        x_regroup(3)
-        x_quantise(2)
-        g_regroup(1, 0, 4, 0, P, "v")
-        x_quantise(3)
-        g_regroup(1, 4, 8, 0, P, "v")
-        g_regroup(1, 8, 9, 0, P, "v")
-        g_quantise(1, 0, 8)
-        g_quantise(1, 8, 9)
 
         for ob in GPSIMD_BLOCKS:
             for s0 in (0, 4):
@@ -138,16 +126,31 @@ def tile_locallyconnected2d_kernel(tc, x, weight, grad_out, out):
                     g_regroup(ob, s0, s0 + 4, o0, o0 + 64, "g")
             g_regroup(ob, 8, 9, 0, P, "g")
 
-        quantised = [0, 1]
-        count = {"s": 0, "v": 0}
+        prep = {
+            (0, 2): ((g_quantise, (0, 4, 8)),),
+            (0, 4): ((g_quantise, (0, 8, 9)), (x_regroup, (1,))),
+            (0, 6): ((x_quantise, (1,)),),
+            (1, 2): ((x_regroup, (2,)),),
+            (1, 5): ((x_quantise, (2,)),),
+            (2, 1): ((x_regroup, (3,)),),
+            (2, 4): ((x_quantise, (3,)),),
+            (1, 7): ((g_regroup, (1, 0, 4, 0, P, "v")),),
+            (2, 6): ((g_regroup, (1, 4, 8, 0, P, "v")),),
+            (2, 8): ((g_quantise, (1, 0, 4)),),
+            (3, 2): ((g_regroup, (1, 8, 9, 0, P, "v")),),
+            (3, 5): ((g_quantise, (1, 4, 8)),),
+            (3, 8): ((g_quantise, (1, 8, 9)),),
+        }
+        for ob in (2, 3):
+            first = 4 * ob - 4
+            prep[(first, 2)] = ((g_regroup, (ob, 0, 4, 0, P, "v")),)
+            prep[(first + 1, 2)] = ((g_regroup, (ob, 4, 8, 0, P, "v")),)
+            prep[(first + 1, 6)] = ((g_quantise, (ob, 0, 4)),)
+            prep[(first + 2, 2)] = ((g_regroup, (ob, 8, 9, 0, P, "v")),)
+            prep[(first + 2, 6)] = ((g_quantise, (ob, 4, 8)),)
+            prep[(first + 3, 2)] = ((g_quantise, (ob, 8, 9)),)
 
-        def product(ob, r, place, eng):
-            if ob not in quantised:
-                g_quantise(ob, 0, 8)
-                g_quantise(ob, 8, 9)
-                quantised.append(ob)
-            stage = st[eng][(count[eng] // GRID) % len(st[eng])]
-            count[eng] = count[eng] + 1
+        def product(ob, r, place, eng, stage):
             h, w = divmod(place, 3)
             pool = ps_s if eng == "s" else ps_v
             acc = pool.tile([P, N_PASS], F32, name="acc_" + eng)
@@ -168,15 +171,12 @@ def tile_locallyconnected2d_kernel(tc, x, weight, grad_out, out):
                 nc.scalar.copy(out=dst, in_=src)
             else:
                 nc.vector.tensor_copy(out=dst, in_=src)
-            if place == GRID - 1:
-                nc.sync.dma_start(out=out_v[ob, :, r * CR:(r + 1) * CR, :], in_=stage[:])
 
-        s_units = [(ob, r, place) for ob, r in S_TILES for place in range(GRID)]
-        v_units = [(ob, r, place) for ob, r in V_TILES for place in range(GRID)]
-        for i in range(len(s_units)):
-            ob, r, place = s_units[i]
-            product(ob, r, place, "s")
-            k = i - V_START
-            if 0 <= k < len(v_units):
-                ob, r, place = v_units[k]
-                product(ob, r, place, "v")
+        for i in range(len(TILES)):
+            ob, r = TILES[i]
+            stage = st[i % N_STAGE]
+            for place in range(GRID):
+                for fn, args in prep.get((i, place), ()):
+                    fn(*args)
+                product(ob, r, place, "v" if place in V_SHARE[V_COUNT[i]] else "s", stage)
+            nc.sync.dma_start(out=out_v[ob, :, r * CR:(r + 1) * CR, :], in_=stage[:])

@@ -28,8 +28,8 @@ USED = CR * 12
 FLOPS = 2 * 49 * B * C * O
 BYTES = 2 * B * XCOLS + 2 * B * O * GRID + 4 * O * C * RUN
 
-N_STAGE = 6
-S_ZEROED = 3
+N_STAGE = 5
+S_ZEROED = 2
 TILES = tuple((ob, r) for ob in range(OBLOCKS) for r in range(NR))
 V_SHARE = {1: (5,), 2: (3, 7), 3: (1, 4, 7), 4: (1, 3, 5, 7), 5: (0, 2, 4, 6, 8)}
 V_COUNT = (1, 2, 1, 2) + (3, 4) * 4 + (4, 5) * 2
@@ -48,7 +48,8 @@ def tile_locallyconnected2d_kernel(tc, x, weight, grad_out, out):
         ps_v = ctx.enter_context(tc.psum_pool(name="ps_v", bufs=3))
         ctx.enter_context(tc.manual_schedule())
 
-        xraw = keep.tile([P, PACK, XCOLS], BF16, name="xraw")
+        xraw0 = keep.tile([P, PACK, XR], BF16, name="xraw0")
+        xraw1 = keep.tile([P, PACK, XCOLS - XR], BF16, name="xraw1")
         xg = keep.tile([P, NR, N_PASS, PACK], BF16, name="xg", align_bytes=64)
         xc = keep.tile([P, NR * N_PASS], U32, name="xc", align_bytes=64)
         xs = keep.tile([P, NR * N_PASS], U8, name="xs", align_bytes=64)
@@ -67,18 +68,21 @@ def tile_locallyconnected2d_kernel(tc, x, weight, grad_out, out):
             t = keep.tile([P, CR, RUN], F32, name="st%d" % i)
             st.append(t)
 
-        nc.sync.dma_start(out=xraw[:, :, 0:XR], in_=x_v[:, :, 0:XR])
+        nc.sync.dma_start(out=xraw0[:], in_=x_v[:, :, 0:XR])
         nc.sync.dma_start(out=graw[0][:], in_=g_v[:, :, 0:GCOLS])
-        nc.sync.dma_start(out=xraw[:, :, XR:XCOLS], in_=x_v[:, :, XR:XCOLS])
+        nc.sync.dma_start(out=xraw1[:], in_=x_v[:, :, XR:XCOLS])
         for ob in range(1, OBLOCKS):
             nc.sync.dma_start(out=graw[ob][:], in_=g_v[:, :, ob * GCOLS:(ob + 1) * GCOLS])
 
         for r in range(NR):
             nc.gpsimd.memset(xg[:, r, :, :].rearrange("p n j -> p (n j)").bitcast(F32), 0.0)
         nc.vector.memset(zero[:], 0.0)
-        for t in st[S_ZEROED:]:
-            nc.vector.memset(t[:, :, 0:21], 0.0)
-            nc.vector.memset(t[:, :, 60:81], 0.0)
+        def v_zero(i, lo):
+            nc.vector.memset(st[i][:, :, lo:lo + 21], 0.0)
+
+        for i in (2, 3):
+            v_zero(i, 0)
+            v_zero(i, 60)
         zsrc = zero[:].unsqueeze(1).to_broadcast([P, CR, 21])
         for t in st[:S_ZEROED]:
             nc.scalar.copy(out=t[:, :, 0:21], in_=zsrc)
@@ -86,7 +90,8 @@ def tile_locallyconnected2d_kernel(tc, x, weight, grad_out, out):
 
         def x_regroup(r):
             dst = xg[:, r, 0:USED, :].rearrange("p (q k) j -> p q k j", k=4)[:, :, 1:4, :]
-            src = xraw[:, :, r * XR:(r + 1) * XR].rearrange("p j (q w) -> p q j w", w=3)
+            raw = xraw0[:] if r == 0 else xraw1[:, :, (r - 1) * XR:r * XR]
+            src = raw.rearrange("p j (q w) -> p q j w", w=3)
             nc.vector.tensor_copy(out=dst.rearrange("p q k j -> p q j k"), in_=src)
 
         def x_quantise(r):
@@ -130,6 +135,8 @@ def tile_locallyconnected2d_kernel(tc, x, weight, grad_out, out):
             (0, 2): ((g_quantise, (0, 4, 8)),),
             (0, 4): ((g_quantise, (0, 8, 9)), (x_regroup, (1,))),
             (0, 6): ((x_quantise, (1,)),),
+            (0, 8): ((v_zero, (4, 0)),),
+            (1, 1): ((v_zero, (4, 60)),),
             (1, 2): ((x_regroup, (2,)),),
             (1, 5): ((x_quantise, (2,)),),
             (2, 1): ((x_regroup, (3,)),),

from contextlib import ExitStack

import concourse.mybir as mybir

F32 = mybir.dt.float32
BF16 = mybir.dt.bfloat16
U32 = mybir.dt.uint32
U8 = mybir.dt.uint8
E4X4 = mybir.dt.float8_e4m3fn_x4
E5X4 = mybir.dt.float8_e5m2_x4
MULT = mybir.AluOpType.mult
ADD = mybir.AluOpType.add

P = 128
PACK = 4
B, C, O = 512, 128, 512
GRID = 9
RUN = GRID * GRID
XCOLS = C * GRID
GCOLS = P * GRID
OBLOCKS = O // P
N_PASS = 512
CR = 32
NR = C // CR
XR = CR * GRID
USED = CR * 12

FLOPS = 2 * 49 * B * C * O
BYTES = 2 * B * XCOLS + 2 * B * O * GRID + 4 * O * C * RUN

N_STAGE = 5
S_ZEROED = 2
TILES = tuple((ob, r) for ob in range(OBLOCKS) for r in range(NR))
V_SHARE = {1: (5,), 2: (3, 7), 3: (1, 4, 7), 4: (1, 3, 5, 7), 5: (0, 2, 4, 6, 8)}
V_COUNT = (1, 2, 1, 2) + (3, 4) * 4 + (4, 5) * 2
GPSIMD_BLOCKS = ()


def tile_locallyconnected2d_kernel(tc, x, weight, grad_out, out):
    nc = tc.nc
    x_v = x.rearrange("(p j) c h w -> p j (c h w)", j=PACK)
    g_v = grad_out.rearrange("(p j) o h w -> p j (o h w)", j=PACK)
    out_v = out.rearrange("a (b o) c h w t -> (a b) o c (h w t)", o=P)

    with ExitStack() as ctx:
        keep = ctx.enter_context(tc.tile_pool(name="keep", bufs=1))
        ps_s = ctx.enter_context(tc.psum_pool(name="ps_s", bufs=5))
        ps_v = ctx.enter_context(tc.psum_pool(name="ps_v", bufs=3))
        ctx.enter_context(tc.manual_schedule())

        xraw0 = keep.tile([P, PACK, XR], BF16, name="xraw0")
        xraw1 = keep.tile([P, PACK, XCOLS - XR], BF16, name="xraw1")
        xg = keep.tile([P, NR, N_PASS, PACK], BF16, name="xg", align_bytes=64)
        xc = keep.tile([P, NR * N_PASS], U32, name="xc", align_bytes=64)
        xs = keep.tile([P, NR * N_PASS], U8, name="xs", align_bytes=64)
        gc = keep.tile([P, OBLOCKS, GCOLS], U32, name="gc", align_bytes=64)
        gs = keep.tile([P, OBLOCKS, GCOLS], U8, name="gs", align_bytes=64)
        zero = keep.tile([P, 21], F32, name="zero")
        graw = []
        gg = []
        for ob in range(OBLOCKS):
            t = keep.tile([P, PACK, GCOLS], BF16, name="graw%d" % ob)
            graw.append(t)
            t = keep.tile([P, GRID, P, PACK], BF16, name="gg%d" % ob, align_bytes=64)
            gg.append(t)
        st = []
        for i in range(N_STAGE):
            t = keep.tile([P, CR, RUN], F32, name="st%d" % i)
            st.append(t)

        nc.sync.dma_start(out=xraw0[:], in_=x_v[:, :, 0:XR])
        nc.sync.dma_start(out=graw[0][:], in_=g_v[:, :, 0:GCOLS])
        nc.sync.dma_start(out=xraw1[:], in_=x_v[:, :, XR:XCOLS])
        for ob in range(1, OBLOCKS):
            nc.sync.dma_start(out=graw[ob][:], in_=g_v[:, :, ob * GCOLS:(ob + 1) * GCOLS])

        for r in range(NR):
            nc.gpsimd.memset(xg[:, r, :, :].rearrange("p n j -> p (n j)").bitcast(F32), 0.0)
        nc.vector.memset(zero[:], 0.0)
        def v_zero(i, lo):
            nc.vector.memset(st[i][:, :, lo:lo + 21], 0.0)

        for i in (2, 3):
            v_zero(i, 0)
            v_zero(i, 60)
        zsrc = zero[:].unsqueeze(1).to_broadcast([P, CR, 21])
        for t in st[:S_ZEROED]:
            nc.scalar.copy(out=t[:, :, 0:21], in_=zsrc)
            nc.scalar.copy(out=t[:, :, 60:81], in_=zsrc)

        def x_regroup(r):
            dst = xg[:, r, 0:USED, :].rearrange("p (q k) j -> p q k j", k=4)[:, :, 1:4, :]
            raw = xraw0[:] if r == 0 else xraw1[:, :, (r - 1) * XR:r * XR]
            src = raw.rearrange("p j (q w) -> p q j w", w=3)
            nc.vector.tensor_copy(out=dst.rearrange("p q k j -> p q j k"), in_=src)

        def x_quantise(r):
            nc.vector.quantize_mx(
                out=xc[:, r * N_PASS:(r + 1) * N_PASS].bitcast(E4X4),
                scales=xs[:, r * N_PASS:(r + 1) * N_PASS],
                in_=xg[:, r, :, :].rearrange("p n j -> p (n j)"),
            )

        def g_regroup(ob, s0, s1, o0, o1, eng):
            dst = gg[ob][:, s0:s1, o0:o1, :].rearrange("p s o j -> p o j s")
            src = graw[ob][:].rearrange("p j (o s) -> p o j s", s=GRID)[:, o0:o1, :, s0:s1]
            if eng == "v":
                nc.vector.tensor_copy(out=dst, in_=src)
            elif eng == "s":
                nc.scalar.copy(out=dst, in_=src)
            else:
                nc.gpsimd.tensor_scalar(out=dst, in0=src, scalar1=1.0, scalar2=0.0, op0=MULT, op1=ADD)

        def g_quantise(ob, s0, s1):
            nc.vector.quantize_mx(
                out=gc[:, ob, s0 * P:s1 * P].bitcast(E5X4),
                scales=gs[:, ob, s0 * P:s1 * P],
                in_=gg[ob][:, s0:s1, :, :].rearrange("p s o j -> p (s o j)"),
            )

        x_regroup(0)
        x_quantise(0)
        g_regroup(0, 0, 4, 0, P, "v")
        g_regroup(0, 4, 8, 0, P, "s")
        g_regroup(0, 8, 9, 0, P, "s")
        g_quantise(0, 0, 4)

        for ob in GPSIMD_BLOCKS:
            for s0 in (0, 4):
                for o0 in (0, 64):
                    g_regroup(ob, s0, s0 + 4, o0, o0 + 64, "g")
            g_regroup(ob, 8, 9, 0, P, "g")

        prep = {
            (0, 2): ((g_quantise, (0, 4, 8)),),
            (0, 4): ((g_quantise, (0, 8, 9)), (x_regroup, (1,))),
            (0, 6): ((x_quantise, (1,)),),
            (0, 8): ((v_zero, (4, 0)),),
            (1, 1): ((v_zero, (4, 60)),),
            (1, 2): ((x_regroup, (2,)),),
            (1, 5): ((x_quantise, (2,)),),
            (2, 1): ((x_regroup, (3,)),),
            (2, 4): ((x_quantise, (3,)),),
            (1, 7): ((g_regroup, (1, 0, 4, 0, P, "v")),),
            (2, 6): ((g_regroup, (1, 4, 8, 0, P, "v")),),
            (2, 8): ((g_quantise, (1, 0, 4)),),
            (3, 2): ((g_regroup, (1, 8, 9, 0, P, "v")),),
            (3, 5): ((g_quantise, (1, 4, 8)),),
            (3, 8): ((g_quantise, (1, 8, 9)),),
        }
        for ob in (2, 3):
            first = 4 * ob - 4
            prep[(first, 2)] = ((g_regroup, (ob, 0, 4, 0, P, "v")),)
            prep[(first + 1, 2)] = ((g_regroup, (ob, 4, 8, 0, P, "v")),)
            prep[(first + 1, 6)] = ((g_quantise, (ob, 0, 4)),)
            prep[(first + 2, 2)] = ((g_regroup, (ob, 8, 9, 0, P, "v")),)
            prep[(first + 2, 6)] = ((g_quantise, (ob, 4, 8)),)
            prep[(first + 3, 2)] = ((g_quantise, (ob, 8, 9)),)

        def product(ob, r, place, eng, stage):
            h, w = divmod(place, 3)
            pool = ps_s if eng == "s" else ps_v
            acc = pool.tile([P, N_PASS], F32, name="acc_" + eng)
            nc.tensor.matmul_mx(
                out=acc[:],
                lhsT=gc[:, ob, place * P:(place + 1) * P].bitcast(E5X4),
                lhsT_scale=gs[:, ob, place * P:(place + 1) * P],
                rhs=xc[:, r * N_PASS:(r + 1) * N_PASS].bitcast(E4X4),
                rhs_scale=xs[:, r * N_PASS:(r + 1) * N_PASS],
                start=True,
                stop=True,
            )
            a_lo, a_hi, t_lo = ((0, 2, 3), (0, 3, 0), (1, 3, 0))[h]
            src = acc[:, w:w + USED].rearrange("p (c a k) -> p c a k", a=3, k=4)[:, :, a_lo:a_hi, 0:3]
            first = place * GRID + t_lo
            dst = stage[:, :, first:first + 3 * (a_hi - a_lo)].rearrange("p c (a k) -> p c a k", k=3)
            if eng == "s":
                nc.scalar.copy(out=dst, in_=src)
            else:
                nc.vector.tensor_copy(out=dst, in_=src)

        for i in range(len(TILES)):
            ob, r = TILES[i]
            stage = st[i % N_STAGE]
            for place in range(GRID):
                for fn, args in prep.get((i, place), ()):
                    fn(*args)
                product(ob, r, place, "v" if place in V_SHARE[V_COUNT[i]] else "s", stage)
            nc.sync.dma_start(out=out_v[ob, :, r * CR:(r + 1) * CR, :], in_=stage[:])
